import numpy as np
import ml_dtypes


def mxq(x, axis, fmt="e4m3"):
    dtype, down = {"e4m3": (ml_dtypes.float8_e4m3fn, 7), "e5m2": (ml_dtypes.float8_e5m2, 14)}[fmt]
    v = np.moveaxis(np.asarray(x, np.float32).astype(ml_dtypes.bfloat16).astype(np.float64), axis, -1)
    blocks = v.reshape(v.shape[:-1] + (-1, 32))
    amax = np.abs(blocks).max(-1, keepdims=True)
    byte = np.maximum(np.where(amax > 0, np.frexp(amax)[1] - 1 + 127, 0) - down, 1)
    scale = np.exp2(byte - 127.0)
    codes = (blocks / scale).astype(np.float32).astype(dtype).astype(np.float64)
    return np.moveaxis((codes * scale).reshape(v.shape), -1, axis)


WIDE = False


def mx_kscale(k):
    if not WIDE:
        return np.ones(k)
    levels = np.array([10, -10, 5, -5, 0])
    a = np.random.permutation(np.resize(levels, k // 512 * 4)).reshape(k // 512, 4)
    idx = np.arange(k)
    return np.exp2(a[idx // 512, idx % 128 // 32])


BF16 = ml_dtypes.bfloat16


def bf(x):
    return np.asarray(x, np.float32).astype(BF16)


def f64(x):
    return np.asarray(x).astype(np.float64)


E2M1 = np.array([0.0, 0.5, 1.0, 1.5, 2.0, 3.0, 4.0, 6.0, -0.0, -0.5, -1.0, -1.5, -2.0, -3.0, -4.0, -6.0])


def pack_weight(w, fmt):
    k, n = w.shape
    w = f64(bf(w)).reshape(k // 32, 32, n)
    amax = np.abs(w).max(1)
    if fmt == "e4m3":
        byte = np.frexp(amax)[1] - 1 + 127 - 7
    else:
        mant, ex = np.frexp(amax / 6.0)
        byte = np.where(mant > 0.5, ex, ex - 1) + 127
    byte = np.clip(np.where(amax > 0, byte, 1), 1, 254)
    scaled = (w * np.exp2(127.0 - byte)[:, None, :]).reshape(k, n).astype(np.float32)
    by_word = np.ascontiguousarray(scaled.reshape(k // 512, 128, 4, n).transpose(0, 1, 3, 2))
    if fmt == "e4m3":
        words = by_word.astype(ml_dtypes.float8_e4m3fn).view(np.uint8)
    else:
        c = by_word.astype(ml_dtypes.float4_e2m1fn).view(np.uint8) & 0xF
        words = c[..., 0::2] | (c[..., 1::2] << 4)
    return np.ascontiguousarray(words), np.ascontiguousarray(byte.astype(np.uint8).reshape(k // 512, 16, n))


def unpack_weight(words, scales, fmt):
    g, p, n, _ = words.shape
    if fmt == "e4m3":
        vals = np.ascontiguousarray(words).view(ml_dtypes.float8_e4m3fn).astype(np.float64)
    else:
        nib = np.empty((g, p, n, 4), np.uint8)
        nib[..., 0::2] = words & 0xF
        nib[..., 1::2] = words >> 4
        vals = E2M1[nib]
    vals = vals * np.repeat(np.exp2(scales.astype(np.float64) - 127.0), 8, axis=1)[..., None]
    return vals.transpose(0, 1, 3, 2).reshape(g * 512, n)

def pack4(w):
    words, scales = pack_weight(w, "e2m1")
    return words.reshape(words.shape[0], 128, -1), scales


def unpack4(words, scales):
    return unpack_weight(words.reshape(words.shape[0], 128, -1, 2), scales, "e2m1")


S, D, N_HEADS, N_KV_HEADS, HEAD_DIM = 8192, 512, 2, 1, 64
Q_DIM = N_HEADS * HEAD_DIM
KV_DIM = N_KV_HEADS * HEAD_DIM
ROPE_THETA = 500000.0


def apply_rope(t, cos, sin):
    te = t[:, :, ::2]
    to = t[:, :, 1::2]
    c = cos[:, None, :]
    s = sin[:, None, :]
    te_rot = te * c - to * s
    to_rot = te * s + to * c
    return np.stack([te_rot, to_rot], axis=-1).reshape(t.shape)


def setup_inputs():
    s = mx_kscale(D)
    inv_freq = 1.0 / ROPE_THETA ** (np.arange(0, HEAD_DIM, 2) / HEAD_DIM)
    angles = np.arange(S)[:, None] * inv_freq[None, :]
    x = bf(np.random.standard_normal((S, D)) * s)
    freqs_cos = bf(np.cos(angles))
    freqs_sin = bf(np.sin(angles))
    wqkv = np.random.standard_normal((Q_DIM + 2 * KV_DIM, D)) / np.sqrt(D) / s[None, :]
    words, scales = pack4(np.ascontiguousarray(wqkv.T))
    return {"x": x,
            "freqs_cos": freqs_cos,
            "freqs_sin": freqs_sin,
            "wqkv_words": words,
            "wqkv_scales": scales}


def reference(x, freqs_cos, freqs_sin, wqkv_words, wqkv_scales):
    qkv = mxq(f64(x), 1, "e4m3") @ unpack4(wqkv_words, wqkv_scales)
    q = qkv[:, :Q_DIM].reshape(S, N_HEADS, HEAD_DIM)
    k = qkv[:, Q_DIM:Q_DIM + KV_DIM].reshape(S, N_KV_HEADS, HEAD_DIM)
    v = qkv[:, Q_DIM + KV_DIM:].reshape(S, N_KV_HEADS, HEAD_DIM)
    cos, sin = f64(freqs_cos), f64(freqs_sin)
    return apply_rope(q, cos, sin), apply_rope(k, cos, sin), v

@@ -1,0 +1,204 @@
+from contextlib import ExitStack
+
+import concourse.mybir as mybir
+from concourse.masks import make_identity
+
+F32 = mybir.dt.float32
+BF16 = mybir.dt.bfloat16
+I32 = mybir.dt.int32
+U32 = mybir.dt.uint32
+U8 = mybir.dt.uint8
+FP8X4 = mybir.dt.float8_e4m3fn_x4
+FP4X4 = mybir.dt.float4_e2m1fn_x4
+MULT = mybir.AluOpType.mult
+ADD = mybir.AluOpType.add
+
+P = 128
+ROWS = 8192
+K = 512
+K_WORDS = K // 2
+Q_COLS, K_COLS, V_COLS = 128, 64, 64
+QKV_COLS = Q_COLS + K_COLS + V_COLS
+ROT_COLS = Q_COLS + K_COLS
+HEADS = 3
+PAIRS = 32
+ROT_PAIRS = HEADS * PAIRS
+Q_PAIRS = Q_COLS // 2
+
+TILES = ROWS // P
+BANK_TILES = 2
+GROUP_BANKS = 2
+GROUP = GROUP_BANKS * BANK_TILES
+GROUPS = TILES // GROUP
+UNIT_GROUPS = 2
+UNIT = UNIT_GROUPS * GROUP
+UNITS = TILES // UNIT
+
+FLOPS = 2 * ROWS * K * QKV_COLS
+
+
+def tile_mha_pa_t_kernel(
+    tc, x, freqs_cos, freqs_sin, wqkv_words, wqkv_scales, out_0, out_1, out_2
+):
+    nc = tc.nc
+    x_rows = x.rearrange("(p t) k -> p t k", t=TILES)
+    cos_rows = freqs_cos.rearrange("(p t) i -> p t i", t=TILES)
+    sin_rows = freqs_sin.rearrange("(p t) i -> p t i", t=TILES)
+    q_rows = out_0.rearrange("(p t) h d -> p t (h d)", t=TILES)
+    k_rows = out_1.rearrange("(p t) h d -> p t (h d)", t=TILES)
+    v_rows = out_2.rearrange("(p t) h d -> p t (h d)", t=TILES)
+
+    with ExitStack() as stack:
+        const = stack.enter_context(tc.tile_pool(name="const", bufs=1))
+        x_pool = stack.enter_context(tc.tile_pool(name="x", bufs=GROUPS))
+        stage = stack.enter_context(tc.tile_pool(name="stage", bufs=3))
+        terms = stack.enter_context(tc.tile_pool(name="terms", bufs=3))
+        results = stack.enter_context(tc.tile_pool(name="results", bufs=UNITS))
+        xt_pool = stack.enter_context(tc.psum_pool(name="xt", bufs=2 * GROUP_BANKS))
+        qkv_pool = stack.enter_context(tc.psum_pool(name="qkv", bufs=2 * GROUP_BANKS))
+        stack.enter_context(tc.manual_schedule())
+
+        identity = const.tile([P, P], F32, name="identity")
+        make_identity(nc, identity[:])
+
+        w_words = const.tile([P, 2 * QKV_COLS], U8, name="w_words", align_bytes=64)
+        w_scales = const.tile([P, QKV_COLS], U8, name="w_scales", align_bytes=64)
+        nc.vector.memset(w_scales[:].bitcast(I32), 0)
+
+        cos_sb = const.tile([P, TILES, PAIRS], BF16, name="cos_sb")
+        sin_sb = const.tile([P, TILES, PAIRS], BF16, name="sin_sb")
+        neg_sin_sb = const.tile([P, TILES, PAIRS], BF16, name="neg_sin_sb")
+
+        x_groups = []
+        for g in range(GROUPS):
+            x_group = x_pool.tile([P, GROUP, K], BF16, name="x_group")
+            x_groups.append(x_group)
+
+        def load_x(g):
+            nc.sync.dma_start(out=x_groups[g][:], in_=x_rows[:, g * GROUP : (g + 1) * GROUP, :])
+
+        load_x(0)
+        load_x(1)
+        nc.sync.dma_start(out=w_words[:].bitcast(I32), in_=wqkv_words[0].bitcast(I32))
+        for r in range(4):
+            nc.sync.dma_start(
+                out=w_scales[r:P:32, :].bitcast(I32), in_=wqkv_scales[0, r:16:4, :].bitcast(I32)
+            )
+        nc.sync.dma_start(out=cos_sb[:], in_=cos_rows)
+        nc.sync.dma_start(out=sin_sb[:], in_=sin_rows)
+        for g in range(2, GROUPS):
+            load_x(g)
+
+        def transpose_group(g):
+            words = x_groups[g][:].bitcast(F32)
+            grouped = stage.tile([P, GROUP * K], BF16, name="grouped", align_bytes=64)
+            grouped_words = grouped[:].bitcast(F32)
+            bank_words = BANK_TILES * K_WORDS
+            for b in range(GROUP_BANKS):
+                xt = xt_pool.tile([P, BANK_TILES, 2, P], F32, name="xt")
+                for j in range(BANK_TILES):
+                    for half in range(2):
+                        nc.tensor.transpose(
+                            out=xt[:, j, half, :],
+                            in_=words[:, b * BANK_TILES + j, half:K_WORDS:2],
+                            identity=identity[:],
+                        )
+                nc.scalar.copy(
+                    out=grouped_words[:, b * bank_words : (b + 1) * bank_words].rearrange(
+                        "p (j r half) -> p j r half", j=BANK_TILES, half=2
+                    ),
+                    in_=xt[:].rearrange("p j half r -> p j r half"),
+                )
+            return grouped
+
+        def project_group(g, grouped, v_sb):
+            codes = stage.tile([P, GROUP * P], U32, name="codes", align_bytes=64)
+            scales = stage.tile([P, GROUP * P], U8, name="scales", align_bytes=64)
+            nc.vector.quantize_mx(out=codes[:].bitcast(FP8X4), scales=scales[:], in_=grouped[:])
+            banks = []
+            for b in range(GROUP_BANKS):
+                qkv = qkv_pool.tile([P, BANK_TILES, QKV_COLS], F32, name="qkv")
+                for j in range(BANK_TILES):
+                    rows = slice((b * BANK_TILES + j) * P, (b * BANK_TILES + j + 1) * P)
+                    nc.tensor.matmul_mx(
+                        out=qkv[:, j, :],
+                        lhsT=codes[:, rows].bitcast(FP8X4),
+                        lhsT_scale=scales[:, rows],
+                        rhs=w_words[:].bitcast(FP4X4),
+                        rhs_scale=w_scales[:],
+                        start=True,
+                        stop=True,
+                    )
+                banks.append(qkv)
+            for b in range(GROUP_BANKS):
+                first = (g % UNIT_GROUPS) * GROUP + b * BANK_TILES
+                nc.scalar.copy(
+                    out=v_sb[:, first : first + BANK_TILES, :], in_=banks[b][:, :, ROT_COLS:QKV_COLS]
+                )
+            tiles = slice(g * GROUP, (g + 1) * GROUP)
+            nc.scalar.mul(out=neg_sin_sb[:, tiles, :], in_=sin_sb[:, tiles, :], mul=-1.0)
+            return banks
+
+        def multiply_group(g, banks, cos_terms, sin_terms):
+            for b in range(GROUP_BANKS):
+                qkv = banks[b]
+                in_table = slice(g * GROUP + b * BANK_TILES, g * GROUP + (b + 1) * BANK_TILES)
+                first = (g % UNIT_GROUPS) * GROUP + b * BANK_TILES
+                in_unit = slice(first, first + BANK_TILES)
+                even = qkv[:, :, 0:ROT_COLS:2]
+                odd = qkv[:, :, 1:ROT_COLS:2]
+                for out_plane, features, table in (
+                    (cos_terms[:, 0], even, cos_sb),
+                    (cos_terms[:, 1], odd, cos_sb),
+                    (sin_terms[:, 1], even, sin_sb),
+                    (sin_terms[:, 0], odd, neg_sin_sb),
+                ):
+                    nc.vector.tensor_tensor(
+                        out=out_plane[:, in_unit, :].rearrange("p j (h i) -> p j h i", h=HEADS),
+                        in0=features.rearrange("p j (h i) -> p j h i", h=HEADS),
+                        in1=table[:, in_table, :]
+                        .unsqueeze(2)
+                        .to_broadcast([P, BANK_TILES, HEADS, PAIRS]),
+                        op=MULT,
+                    )
+
+        def add_and_store(u, cos_terms, sin_terms, v_sb):
+            adder = nc.vector if u == UNITS - 1 else nc.gpsimd
+            tiles = slice(u * UNIT, (u + 1) * UNIT)
+            q_sb = results.tile([P, UNIT, Q_COLS], F32, name="q_sb")
+            k_sb = results.tile([P, UNIT, K_COLS], F32, name="k_sb")
+            for out_sb, pairs, out_rows in (
+                (q_sb, slice(0, Q_PAIRS), q_rows),
+                (k_sb, slice(Q_PAIRS, ROT_PAIRS), k_rows),
+            ):
+                adder.tensor_tensor(
+                    out=out_sb[:].rearrange("p t (n e) -> p t n e", e=2),
+                    in0=cos_terms[:, :, :, pairs].rearrange("p e t n -> p t n e"),
+                    in1=sin_terms[:, :, :, pairs].rearrange("p e t n -> p t n e"),
+                    op=ADD,
+                )
+                nc.sync.dma_start(out=out_rows[:, tiles, :], in_=out_sb[:])
+            nc.sync.dma_start(out=v_rows[:, tiles, :], in_=v_sb[:])
+
+        grouped_of = {}
+        banks_of = {}
+        v_of = {}
+        terms_of = {}
+        for step in range(GROUPS + 2):
+            if step < GROUPS:
+                grouped_of[step] = transpose_group(step)
+            g = step - 1
+            if 0 <= g < GROUPS:
+                if g % UNIT_GROUPS == 0:
+                    v_of[g // UNIT_GROUPS] = results.tile([P, UNIT, V_COLS], F32, name="v_sb")
+                banks_of[g] = project_group(g, grouped_of[g], v_of[g // UNIT_GROUPS])
+            g = step - 2
+            if 0 <= g:
+                u = g // UNIT_GROUPS
+                if g % UNIT_GROUPS == 0:
+                    cos_terms = terms.tile([P, 2, UNIT, ROT_PAIRS], F32, name="cos_terms")
+                    sin_terms = terms.tile([P, 2, UNIT, ROT_PAIRS], F32, name="sin_terms")
+                    terms_of[u] = (cos_terms, sin_terms)
+                multiply_group(g, banks_of[g], terms_of[u][0], terms_of[u][1])
+                if g % UNIT_GROUPS == UNIT_GROUPS - 1:
+                    add_and_store(u, terms_of[u][0], terms_of[u][1], v_of[u])

@@ -65,9 +65,7 @@ def tile_mha_pa_t_kernel(
         w_scales = const.tile([P, QKV_COLS], U8, name="w_scales", align_bytes=64)
         nc.vector.memset(w_scales[:].bitcast(I32), 0)
 
-        cos_sb = const.tile([P, TILES, PAIRS], BF16, name="cos_sb")
-        sin_sb = const.tile([P, TILES, PAIRS], BF16, name="sin_sb")
-        neg_sin_sb = const.tile([P, TILES, PAIRS], BF16, name="neg_sin_sb")
+        table = const.tile([P, 4, TILES, PAIRS], BF16, name="table")
 
         x_groups = []
         for g in range(GROUPS):
@@ -84,8 +82,8 @@ def tile_mha_pa_t_kernel(
             nc.sync.dma_start(
                 out=w_scales[r:P:32, :].bitcast(I32), in_=wqkv_scales[0, r:16:4, :].bitcast(I32)
             )
-        nc.sync.dma_start(out=cos_sb[:], in_=cos_rows)
-        nc.sync.dma_start(out=sin_sb[:], in_=sin_rows)
+        nc.sync.dma_start(out=table[:, 0], in_=cos_rows)
+        nc.sync.dma_start(out=table[:, 1], in_=sin_rows)
         for g in range(2, GROUPS):
             load_x(g)
 
@@ -136,33 +134,31 @@ def tile_mha_pa_t_kernel(
                     out=v_sb[:, first : first + BANK_TILES, :], in_=banks[b][:, :, ROT_COLS:QKV_COLS]
                 )
             tiles = slice(g * GROUP, (g + 1) * GROUP)
-            nc.scalar.mul(out=neg_sin_sb[:, tiles, :], in_=sin_sb[:, tiles, :], mul=-1.0)
+            nc.scalar.mul(out=table[:, 2, tiles, :], in_=table[:, 1, tiles, :], mul=-1.0)
+            nc.scalar.copy(out=table[:, 3, tiles, :], in_=table[:, 0, tiles, :])
             return banks
 
-        def multiply_group(g, banks, cos_terms, sin_terms):
+        def multiply_group(g, banks, shares):
             for b in range(GROUP_BANKS):
-                qkv = banks[b]
-                in_table = slice(g * GROUP + b * BANK_TILES, g * GROUP + (b + 1) * BANK_TILES)
-                first = (g % UNIT_GROUPS) * GROUP + b * BANK_TILES
-                in_unit = slice(first, first + BANK_TILES)
-                even = qkv[:, :, 0:ROT_COLS:2]
-                odd = qkv[:, :, 1:ROT_COLS:2]
-                for out_plane, features, table in (
-                    (cos_terms[:, 0], even, cos_sb),
-                    (cos_terms[:, 1], odd, cos_sb),
-                    (sin_terms[:, 1], even, sin_sb),
-                    (sin_terms[:, 0], odd, neg_sin_sb),
-                ):
+                for j in range(BANK_TILES):
+                    t = g * GROUP + b * BANK_TILES + j
+                    in_unit = t % UNIT
                     nc.vector.tensor_tensor(
-                        out=out_plane[:, in_unit, :].rearrange("p j (h i) -> p j h i", h=HEADS),
-                        in0=features.rearrange("p j (h i) -> p j h i", h=HEADS),
-                        in1=table[:, in_table, :]
-                        .unsqueeze(2)
-                        .to_broadcast([P, BANK_TILES, HEADS, PAIRS]),
+                        out=shares[:, in_unit].rearrange(
+                            "p (h i) e r -> p h i e r", h=HEADS
+                        ),
+                        in0=banks[b][:, j, 0:ROT_COLS]
+                        .rearrange("p (h i e) -> p h i e", h=HEADS, e=2)
+                        .unsqueeze(4)
+                        .to_broadcast([P, HEADS, PAIRS, 2, 2]),
+                        in1=table[:, :, t, :]
+                        .rearrange("p (e r) i -> p i e r", e=2)
+                        .unsqueeze(1)
+                        .to_broadcast([P, HEADS, PAIRS, 2, 2]),
                         op=MULT,
                     )
 
-        def add_and_store(u, cos_terms, sin_terms, v_sb):
+        def add_and_store(u, shares, v_sb):
             adder = nc.vector if u == UNITS - 1 else nc.gpsimd
             tiles = slice(u * UNIT, (u + 1) * UNIT)
             q_sb = results.tile([P, UNIT, Q_COLS], F32, name="q_sb")
@@ -172,9 +168,9 @@ def tile_mha_pa_t_kernel(
                 (k_sb, slice(Q_PAIRS, ROT_PAIRS), k_rows),
             ):
                 adder.tensor_tensor(
-                    out=out_sb[:].rearrange("p t (n e) -> p t n e", e=2),
-                    in0=cos_terms[:, :, :, pairs].rearrange("p e t n -> p t n e"),
-                    in1=sin_terms[:, :, :, pairs].rearrange("p e t n -> p t n e"),
+                    out=out_sb[:].rearrange("p t (n r) -> p t n r", r=2),
+                    in0=shares[:, :, pairs, 0, :],
+                    in1=shares[:, :, pairs, 1, :],
                     op=ADD,
                 )
                 nc.sync.dma_start(out=out_rows[:, tiles, :], in_=out_sb[:])
@@ -196,9 +192,7 @@ def tile_mha_pa_t_kernel(
             if 0 <= g:
                 u = g // UNIT_GROUPS
                 if g % UNIT_GROUPS == 0:
-                    cos_terms = terms.tile([P, 2, UNIT, ROT_PAIRS], F32, name="cos_terms")
-                    sin_terms = terms.tile([P, 2, UNIT, ROT_PAIRS], F32, name="sin_terms")
-                    terms_of[u] = (cos_terms, sin_terms)
-                multiply_group(g, banks_of[g], terms_of[u][0], terms_of[u][1])
+                    terms_of[u] = terms.tile([P, UNIT, ROT_PAIRS, 2, 2], F32, name="shares")
+                multiply_group(g, banks_of[g], terms_of[u])
                 if g % UNIT_GROUPS == UNIT_GROUPS - 1:
-                    add_and_store(u, terms_of[u][0], terms_of[u][1], v_of[u])
+                    add_and_store(u, terms_of[u], v_of[u])

@@ -27,12 +27,15 @@ Q_PAIRS = Q_COLS // 2
 
 TILES = ROWS // P
 BANK_TILES = 2
-GROUP_BANKS = 2
-GROUP = GROUP_BANKS * BANK_TILES
-GROUPS = TILES // GROUP
-UNIT_GROUPS = 2
-UNIT = UNIT_GROUPS * GROUP
-UNITS = TILES // UNIT
+BANKS = TILES // BANK_TILES
+PSUM_SLOTS = 4
+CHUNK_BANKS = (1, 1, 2, 2, 2, 4, 4, 4, 4, 4, 4)
+HEAD_CHUNKS = 5
+CHUNKS = len(CHUNK_BANKS)
+MAX_TILES = max(CHUNK_BANKS) * BANK_TILES
+RUN_BANKS = 2
+LEAD = 3
+TAIL_UNITS = (1, 4, 3)
 
 FLOPS = 2 * ROWS * K * QKV_COLS
 
@@ -48,14 +51,20 @@ def tile_mha_pa_t_kernel(
     k_rows = out_1.rearrange("(p t) h d -> p t (h d)", t=TILES)
     v_rows = out_2.rearrange("(p t) h d -> p t (h d)", t=TILES)
 
+    assert sum(CHUNK_BANKS) == BANKS
+    first_bank = [sum(CHUNK_BANKS[:c]) for c in range(CHUNKS)]
+    chunk_of = [c for c in range(CHUNKS) for b in range(CHUNK_BANKS[c])]
+
+    def tiles_of(c):
+        return slice(first_bank[c] * BANK_TILES, (first_bank[c] + CHUNK_BANKS[c]) * BANK_TILES)
+
     with ExitStack() as stack:
         const = stack.enter_context(tc.tile_pool(name="const", bufs=1))
-        x_pool = stack.enter_context(tc.tile_pool(name="x", bufs=GROUPS))
-        stage = stack.enter_context(tc.tile_pool(name="stage", bufs=3))
+        stage = stack.enter_context(tc.tile_pool(name="stage", bufs=4))
         terms = stack.enter_context(tc.tile_pool(name="terms", bufs=3))
-        results = stack.enter_context(tc.tile_pool(name="results", bufs=UNITS))
-        xt_pool = stack.enter_context(tc.psum_pool(name="xt", bufs=2 * GROUP_BANKS))
-        qkv_pool = stack.enter_context(tc.psum_pool(name="qkv", bufs=2 * GROUP_BANKS))
+        results = stack.enter_context(tc.tile_pool(name="results", bufs=6))
+        xt_pool = stack.enter_context(tc.psum_pool(name="xt", bufs=PSUM_SLOTS))
+        qkv_pool = stack.enter_context(tc.psum_pool(name="qkv", bufs=PSUM_SLOTS))
         stack.enter_context(tc.manual_schedule())
 
         identity = const.tile([P, P], F32, name="identity")
@@ -65,34 +74,52 @@ def tile_mha_pa_t_kernel(
         w_scales = const.tile([P, QKV_COLS], U8, name="w_scales", align_bytes=64)
         nc.vector.memset(w_scales[:].bitcast(I32), 0)
 
-        table = const.tile([P, 4, TILES, PAIRS], BF16, name="table")
+        head_tiles = sum(CHUNK_BANKS[:HEAD_CHUNKS]) * BANK_TILES
+        table_head = const.tile([P, 4, head_tiles, PAIRS], BF16, name="table_head")
+        table_rest = const.tile([P, 4, TILES - head_tiles, PAIRS], BF16, name="table_rest")
 
-        x_groups = []
-        for g in range(GROUPS):
-            x_group = x_pool.tile([P, GROUP, K], BF16, name="x_group")
-            x_groups.append(x_group)
+        def factors_of(c):
+            tiles = tiles_of(c)
+            if c < HEAD_CHUNKS:
+                return table_head[:, :, tiles, :]
+            return table_rest[:, :, tiles.start - head_tiles : tiles.stop - head_tiles, :]
 
-        def load_x(g):
-            nc.sync.dma_start(out=x_groups[g][:], in_=x_rows[:, g * GROUP : (g + 1) * GROUP, :])
+        x_chunks = []
+        for c in range(CHUNKS):
+            x_chunk = const.tile([P, CHUNK_BANKS[c] * BANK_TILES, K], BF16, name="x_chunk%d" % c)
+            x_chunks.append(x_chunk)
 
-        load_x(0)
-        load_x(1)
+        def load_x(c):
+            nc.sync.dma_start(out=x_chunks[c][:], in_=x_rows[:, tiles_of(c), :])
+
         nc.sync.dma_start(out=w_words[:].bitcast(I32), in_=wqkv_words[0].bitcast(I32))
         for r in range(4):
             nc.sync.dma_start(
                 out=w_scales[r:P:32, :].bitcast(I32), in_=wqkv_scales[0, r:16:4, :].bitcast(I32)
             )
-        nc.sync.dma_start(out=table[:, 0], in_=cos_rows)
-        nc.sync.dma_start(out=table[:, 1], in_=sin_rows)
-        for g in range(2, GROUPS):
-            load_x(g)
+        for c in range(3):
+            load_x(c)
+        nc.sync.dma_start(out=table_head[:, 0], in_=cos_rows[:, 0:head_tiles, :])
+        nc.sync.dma_start(out=table_head[:, 1], in_=sin_rows[:, 0:head_tiles, :])
+        for c in range(3, 6):
+            load_x(c)
+        nc.sync.dma_start(out=table_rest[:, 0], in_=cos_rows[:, head_tiles:TILES, :])
+        nc.sync.dma_start(out=table_rest[:, 1], in_=sin_rows[:, head_tiles:TILES, :])
+        for c in range(6, CHUNKS):
+            load_x(c)
 
-        def transpose_group(g):
-            words = x_groups[g][:].bitcast(F32)
-            grouped = stage.tile([P, GROUP * K], BF16, name="grouped", align_bytes=64)
-            grouped_words = grouped[:].bitcast(F32)
-            bank_words = BANK_TILES * K_WORDS
-            for b in range(GROUP_BANKS):
+        grouped_of = {}
+        codes_of = {}
+        scales_of = {}
+        qkv_of = {}
+        v_of = {}
+        done = {"quantized": 0, "projected": 0, "multiplied": 0}
+        bank_words = BANK_TILES * K_WORDS
+
+        def transpose_chunk(c):
+            grouped_of[c] = stage.tile([P, MAX_TILES * K], BF16, name="grouped", align_bytes=64)
+            words = x_chunks[c][:].bitcast(F32)
+            for b in range(CHUNK_BANKS[c]):
                 xt = xt_pool.tile([P, BANK_TILES, 2, P], F32, name="xt")
                 for j in range(BANK_TILES):
                     for half in range(2):
@@ -102,97 +129,110 @@ def tile_mha_pa_t_kernel(
                             identity=identity[:],
                         )
                 nc.scalar.copy(
-                    out=grouped_words[:, b * bank_words : (b + 1) * bank_words].rearrange(
-                        "p (j r half) -> p j r half", j=BANK_TILES, half=2
-                    ),
+                    out=grouped_of[c][:]
+                    .bitcast(F32)[:, b * bank_words : (b + 1) * bank_words]
+                    .rearrange("p (j r half) -> p j r half", j=BANK_TILES, half=2),
                     in_=xt[:].rearrange("p j half r -> p j r half"),
                 )
-            return grouped
 
-        def project_group(g, grouped, v_sb):
-            codes = stage.tile([P, GROUP * P], U32, name="codes", align_bytes=64)
-            scales = stage.tile([P, GROUP * P], U8, name="scales", align_bytes=64)
-            nc.vector.quantize_mx(out=codes[:].bitcast(FP8X4), scales=scales[:], in_=grouped[:])
-            banks = []
-            for b in range(GROUP_BANKS):
-                qkv = qkv_pool.tile([P, BANK_TILES, QKV_COLS], F32, name="qkv")
-                for j in range(BANK_TILES):
-                    rows = slice((b * BANK_TILES + j) * P, (b * BANK_TILES + j + 1) * P)
-                    nc.tensor.matmul_mx(
-                        out=qkv[:, j, :],
-                        lhsT=codes[:, rows].bitcast(FP8X4),
-                        lhsT_scale=scales[:, rows],
-                        rhs=w_words[:].bitcast(FP4X4),
-                        rhs_scale=w_scales[:],
-                        start=True,
-                        stop=True,
-                    )
-                banks.append(qkv)
-            for b in range(GROUP_BANKS):
-                first = (g % UNIT_GROUPS) * GROUP + b * BANK_TILES
-                nc.scalar.copy(
-                    out=v_sb[:, first : first + BANK_TILES, :], in_=banks[b][:, :, ROT_COLS:QKV_COLS]
+        def quantize_chunk(c):
+            columns = CHUNK_BANKS[c] * BANK_TILES * P
+            codes_of[c] = stage.tile([P, MAX_TILES * P], U32, name="codes", align_bytes=64)
+            scales_of[c] = stage.tile([P, MAX_TILES * P], U8, name="scales", align_bytes=64)
+            nc.vector.quantize_mx(
+                out=codes_of[c][:, 0:columns].bitcast(FP8X4),
+                scales=scales_of[c][:, 0:columns],
+                in_=grouped_of[c][:, 0 : 4 * columns],
+            )
+            done["quantized"] = first_bank[c] + CHUNK_BANKS[c]
+            factors = factors_of(c)
+            nc.scalar.mul(out=factors[:, 2], in_=factors[:, 1], mul=-1.0)
+            nc.scalar.copy(out=factors[:, 3], in_=factors[:, 0])
+
+        def project_bank(b):
+            c = chunk_of[b]
+            if b == first_bank[c]:
+                v_of[c] = results.tile([P, MAX_TILES, V_COLS], F32, name="v_sb")
+            qkv = qkv_pool.tile([P, BANK_TILES, QKV_COLS], F32, name="qkv")
+            qkv_of[b] = qkv
+            at = (b - first_bank[c]) * BANK_TILES
+            for j in range(BANK_TILES):
+                rows = slice((at + j) * P, (at + j + 1) * P)
+                nc.tensor.matmul_mx(
+                    out=qkv[:, j, :],
+                    lhsT=codes_of[c][:, rows].bitcast(FP8X4),
+                    lhsT_scale=scales_of[c][:, rows],
+                    rhs=w_words[:].bitcast(FP4X4),
+                    rhs_scale=w_scales[:],
+                    start=True,
+                    stop=True,
                 )
-            tiles = slice(g * GROUP, (g + 1) * GROUP)
-            nc.scalar.mul(out=table[:, 2, tiles, :], in_=table[:, 1, tiles, :], mul=-1.0)
-            nc.scalar.copy(out=table[:, 3, tiles, :], in_=table[:, 0, tiles, :])
-            return banks
+            nc.scalar.copy(out=v_of[c][:, at : at + BANK_TILES, :], in_=qkv[:, :, ROT_COLS:QKV_COLS])
 
-        def multiply_group(g, banks, shares):
-            for b in range(GROUP_BANKS):
-                for j in range(BANK_TILES):
-                    t = g * GROUP + b * BANK_TILES + j
-                    in_unit = t % UNIT
-                    nc.vector.tensor_tensor(
-                        out=shares[:, in_unit].rearrange(
-                            "p (h i) e r -> p h i e r", h=HEADS
-                        ),
-                        in0=banks[b][:, j, 0:ROT_COLS]
-                        .rearrange("p (h i e) -> p h i e", h=HEADS, e=2)
-                        .unsqueeze(4)
-                        .to_broadcast([P, HEADS, PAIRS, 2, 2]),
-                        in1=table[:, :, t, :]
-                        .rearrange("p (e r) i -> p i e r", e=2)
-                        .unsqueeze(1)
-                        .to_broadcast([P, HEADS, PAIRS, 2, 2]),
-                        op=MULT,
-                    )
+        def project_what_fits():
+            while done["projected"] < min(done["quantized"], done["multiplied"] + PSUM_SLOTS):
+                project_bank(done["projected"])
+                done["projected"] += 1
 
-        def add_and_store(u, shares, v_sb):
-            adder = nc.vector if u == UNITS - 1 else nc.gpsimd
-            tiles = slice(u * UNIT, (u + 1) * UNIT)
-            q_sb = results.tile([P, UNIT, Q_COLS], F32, name="q_sb")
-            k_sb = results.tile([P, UNIT, K_COLS], F32, name="k_sb")
+        def multiply_bank(b, shares):
+            c = chunk_of[b]
+            for j in range(BANK_TILES):
+                at = (b - first_bank[c]) * BANK_TILES + j
+                nc.vector.tensor_tensor(
+                    out=shares[:, at].rearrange("p (h i) e r -> p h i e r", h=HEADS),
+                    in0=qkv_of[b][:, j, 0:ROT_COLS]
+                    .rearrange("p (h i e) -> p h i e", h=HEADS, e=2)
+                    .unsqueeze(4)
+                    .to_broadcast([P, HEADS, PAIRS, 2, 2]),
+                    in1=factors_of(c)[:, :, at, :]
+                    .rearrange("p (e r) i -> p i e r", e=2)
+                    .unsqueeze(1)
+                    .to_broadcast([P, HEADS, PAIRS, 2, 2]),
+                    op=MULT,
+                )
+            done["multiplied"] = b + 1
+
+        def store_v(c):
+            n = CHUNK_BANKS[c] * BANK_TILES
+            nc.sync.dma_start(out=v_rows[:, tiles_of(c), :], in_=v_of[c][:, 0:n, :])
+
+        def add_and_store(c, shares, first, n, adder):
+            tiles = slice(first_bank[c] * BANK_TILES + first, first_bank[c] * BANK_TILES + first + n)
+            q_sb = results.tile([P, MAX_TILES, Q_COLS], F32, name="q_sb")
+            k_sb = results.tile([P, MAX_TILES, K_COLS], F32, name="k_sb")
             for out_sb, pairs, out_rows in (
                 (q_sb, slice(0, Q_PAIRS), q_rows),
                 (k_sb, slice(Q_PAIRS, ROT_PAIRS), k_rows),
             ):
                 adder.tensor_tensor(
-                    out=out_sb[:].rearrange("p t (n r) -> p t n r", r=2),
-                    in0=shares[:, :, pairs, 0, :],
-                    in1=shares[:, :, pairs, 1, :],
+                    out=out_sb[:, 0:n, :].rearrange("p t (n r) -> p t n r", r=2),
+                    in0=shares[:, first : first + n, pairs, 0, :],
+                    in1=shares[:, first : first + n, pairs, 1, :],
                     op=ADD,
                 )
-                nc.sync.dma_start(out=out_rows[:, tiles, :], in_=out_sb[:])
-            nc.sync.dma_start(out=v_rows[:, tiles, :], in_=v_sb[:])
+                nc.sync.dma_start(out=out_rows[:, tiles, :], in_=out_sb[:, 0:n, :])
 
-        grouped_of = {}
-        banks_of = {}
-        v_of = {}
-        terms_of = {}
-        for step in range(GROUPS + 2):
-            if step < GROUPS:
-                grouped_of[step] = transpose_group(step)
-            g = step - 1
-            if 0 <= g < GROUPS:
-                if g % UNIT_GROUPS == 0:
-                    v_of[g // UNIT_GROUPS] = results.tile([P, UNIT, V_COLS], F32, name="v_sb")
-                banks_of[g] = project_group(g, grouped_of[g], v_of[g // UNIT_GROUPS])
-            g = step - 2
-            if 0 <= g:
-                u = g // UNIT_GROUPS
-                if g % UNIT_GROUPS == 0:
-                    terms_of[u] = terms.tile([P, UNIT, ROT_PAIRS, 2, 2], F32, name="shares")
-                multiply_group(g, banks_of[g], terms_of[u])
-                if g % UNIT_GROUPS == UNIT_GROUPS - 1:
-                    add_and_store(u, terms_of[u], v_of[u])
+        transpose_chunk(0)
+        transpose_chunk(1)
+        quantize_chunk(0)
+        project_what_fits()
+        transpose_chunk(2)
+        for c in range(CHUNKS):
+            if c + 1 < CHUNKS:
+                quantize_chunk(c + 1)
+            project_what_fits()
+            if c + LEAD < CHUNKS:
+                transpose_chunk(c + LEAD)
+            shares = terms.tile([P, MAX_TILES, ROT_PAIRS, 2, 2], F32, name="shares")
+            for b in range(first_bank[c], first_bank[c] + CHUNK_BANKS[c]):
+                multiply_bank(b, shares)
+                if (b + 1 - first_bank[c]) % RUN_BANKS == 0 or b + 1 == first_bank[c] + CHUNK_BANKS[c]:
+                    project_what_fits()
+            store_v(c)
+            if c + 1 < CHUNKS:
+                add_and_store(c, shares, 0, CHUNK_BANKS[c] * BANK_TILES, nc.gpsimd)
+            else:
+                first = 0
+                for n in TAIL_UNITS:
+                    add_and_store(c, shares, first, n, nc.gpsimd if first == 0 else nc.vector)
+                    first += n

@@ -179,7 +179,7 @@ def tile_mha_pa_t_kernel(
             for j in range(BANK_TILES):
                 at = (b - first_bank[c]) * BANK_TILES + j
                 nc.vector.tensor_tensor(
-                    out=shares[:, at].rearrange("p (h i) e r -> p h i e r", h=HEADS),
+                    out=shares[:, at].rearrange("p e (h i) r -> p h i e r", h=HEADS),
                     in0=qkv_of[b][:, j, 0:ROT_COLS]
                     .rearrange("p (h i e) -> p h i e", h=HEADS, e=2)
                     .unsqueeze(4)
@@ -206,8 +206,8 @@ def tile_mha_pa_t_kernel(
             ):
                 adder.tensor_tensor(
                     out=out_sb[:, 0:n, :].rearrange("p t (n r) -> p t n r", r=2),
-                    in0=shares[:, first : first + n, pairs, 0, :],
-                    in1=shares[:, first : first + n, pairs, 1, :],
+                    in0=shares[:, first : first + n, 0, pairs, :],
+                    in1=shares[:, first : first + n, 1, pairs, :],
                     op=ADD,
                 )
                 nc.sync.dma_start(out=out_rows[:, tiles, :], in_=out_sb[:, 0:n, :])
@@ -223,7 +223,7 @@ def tile_mha_pa_t_kernel(
             project_what_fits()
             if c + LEAD < CHUNKS:
                 transpose_chunk(c + LEAD)
-            shares = terms.tile([P, MAX_TILES, ROT_PAIRS, 2, 2], F32, name="shares")
+            shares = terms.tile([P, MAX_TILES, 2, ROT_PAIRS, 2], F32, name="shares")
             for b in range(first_bank[c], first_bank[c] + CHUNK_BANKS[c]):
                 multiply_bank(b, shares)
                 if (b + 1 - first_bank[c]) % RUN_BANKS == 0 or b + 1 == first_bank[c] + CHUNK_BANKS[c]:

@@ -178,18 +178,19 @@ def tile_mha_pa_t_kernel(
             c = chunk_of[b]
             for j in range(BANK_TILES):
                 at = (b - first_bank[c]) * BANK_TILES + j
-                nc.vector.tensor_tensor(
-                    out=shares[:, at].rearrange("p e (h i) r -> p h i e r", h=HEADS),
-                    in0=qkv_of[b][:, j, 0:ROT_COLS]
-                    .rearrange("p (h i e) -> p h i e", h=HEADS, e=2)
-                    .unsqueeze(4)
-                    .to_broadcast([P, HEADS, PAIRS, 2, 2]),
-                    in1=factors_of(c)[:, :, at, :]
-                    .rearrange("p (e r) i -> p i e r", e=2)
-                    .unsqueeze(1)
-                    .to_broadcast([P, HEADS, PAIRS, 2, 2]),
-                    op=MULT,
-                )
+                for e in range(2):
+                    nc.vector.tensor_tensor(
+                        out=shares[:, at, e].rearrange("p (h i) r -> p h i r", h=HEADS),
+                        in0=qkv_of[b][:, j, 0:ROT_COLS]
+                        .rearrange("p (h i e) -> p h i e", h=HEADS, e=2)[:, :, :, e]
+                        .unsqueeze(3)
+                        .to_broadcast([P, HEADS, PAIRS, 2]),
+                        in1=factors_of(c)[:, 2 * e : 2 * e + 2, at, :]
+                        .rearrange("p r i -> p i r")
+                        .unsqueeze(1)
+                        .to_broadcast([P, HEADS, PAIRS, 2]),
+                        op=MULT,
+                    )
             done["multiplied"] = b + 1
 
         def store_v(c):

@@ -35,7 +35,7 @@ CHUNKS = len(CHUNK_BANKS)
 MAX_TILES = max(CHUNK_BANKS) * BANK_TILES
 RUN_BANKS = 2
 LEAD = 3
-TAIL_UNITS = (1, 4, 3)
+TAIL_UNITS = (5, 3)
 
 FLOPS = 2 * ROWS * K * QKV_COLS
 
@@ -92,12 +92,13 @@ def tile_mha_pa_t_kernel(
         def load_x(c):
             nc.sync.dma_start(out=x_chunks[c][:], in_=x_rows[:, tiles_of(c), :])
 
+        load_x(0)
         nc.sync.dma_start(out=w_words[:].bitcast(I32), in_=wqkv_words[0].bitcast(I32))
         for r in range(4):
             nc.sync.dma_start(
                 out=w_scales[r:P:32, :].bitcast(I32), in_=wqkv_scales[0, r:16:4, :].bitcast(I32)
             )
-        for c in range(3):
+        for c in range(1, 3):
             load_x(c)
         nc.sync.dma_start(out=table_head[:, 0], in_=cos_rows[:, 0:head_tiles, :])
         nc.sync.dma_start(out=table_head[:, 1], in_=sin_rows[:, 0:head_tiles, :])
@@ -113,6 +114,7 @@ def tile_mha_pa_t_kernel(
         scales_of = {}
         qkv_of = {}
         v_of = {}
+        shares_of = {}
         done = {"quantized": 0, "projected": 0, "multiplied": 0}
         bank_words = BANK_TILES * K_WORDS
 
@@ -197,21 +199,21 @@ def tile_mha_pa_t_kernel(
             n = CHUNK_BANKS[c] * BANK_TILES
             nc.sync.dma_start(out=v_rows[:, tiles_of(c), :], in_=v_of[c][:, 0:n, :])
 
-        def add_and_store(c, shares, first, n, adder):
+        def add_and_store(c, first, n, out_rows, adder):
             tiles = slice(first_bank[c] * BANK_TILES + first, first_bank[c] * BANK_TILES + first + n)
-            q_sb = results.tile([P, MAX_TILES, Q_COLS], F32, name="q_sb")
-            k_sb = results.tile([P, MAX_TILES, K_COLS], F32, name="k_sb")
-            for out_sb, pairs, out_rows in (
-                (q_sb, slice(0, Q_PAIRS), q_rows),
-                (k_sb, slice(Q_PAIRS, ROT_PAIRS), k_rows),
-            ):
-                adder.tensor_tensor(
-                    out=out_sb[:, 0:n, :].rearrange("p t (n r) -> p t n r", r=2),
-                    in0=shares[:, first : first + n, 0, pairs, :],
-                    in1=shares[:, first : first + n, 1, pairs, :],
-                    op=ADD,
-                )
-                nc.sync.dma_start(out=out_rows[:, tiles, :], in_=out_sb[:, 0:n, :])
+            if out_rows is q_rows:
+                out_sb = results.tile([P, MAX_TILES, Q_COLS], F32, name="q_sb")
+                pairs = slice(0, Q_PAIRS)
+            else:
+                out_sb = results.tile([P, MAX_TILES, K_COLS], F32, name="k_sb")
+                pairs = slice(Q_PAIRS, ROT_PAIRS)
+            adder.tensor_tensor(
+                out=out_sb[:, 0:n, :].rearrange("p t (n r) -> p t n r", r=2),
+                in0=shares_of[c][:, first : first + n, 0, pairs, :],
+                in1=shares_of[c][:, first : first + n, 1, pairs, :],
+                op=ADD,
+            )
+            nc.sync.dma_start(out=out_rows[:, tiles, :], in_=out_sb[:, 0:n, :])
 
         transpose_chunk(0)
         transpose_chunk(1)
@@ -225,15 +227,20 @@ def tile_mha_pa_t_kernel(
             if c + LEAD < CHUNKS:
                 transpose_chunk(c + LEAD)
             shares = terms.tile([P, MAX_TILES, 2, ROT_PAIRS, 2], F32, name="shares")
+            shares_of[c] = shares
             for b in range(first_bank[c], first_bank[c] + CHUNK_BANKS[c]):
                 multiply_bank(b, shares)
                 if (b + 1 - first_bank[c]) % RUN_BANKS == 0 or b + 1 == first_bank[c] + CHUNK_BANKS[c]:
                     project_what_fits()
             store_v(c)
-            if c + 1 < CHUNKS:
-                add_and_store(c, shares, 0, CHUNK_BANKS[c] * BANK_TILES, nc.gpsimd)
-            else:
-                first = 0
-                for n in TAIL_UNITS:
-                    add_and_store(c, shares, first, n, nc.gpsimd if first == 0 else nc.vector)
-                    first += n
+            n = CHUNK_BANKS[c] * BANK_TILES
+            if c < CHUNKS - 1:
+                add_and_store(c, 0, n, q_rows, nc.gpsimd)
+            if c < CHUNKS - 2:
+                add_and_store(c, 0, n, k_rows, nc.gpsimd)
+        add_and_store(CHUNKS - 2, 0, CHUNK_BANKS[CHUNKS - 2] * BANK_TILES, k_rows, nc.vector)
+        first = 0
+        for n in TAIL_UNITS:
+            add_and_store(CHUNKS - 1, first, n, q_rows, nc.vector)
+            add_and_store(CHUNKS - 1, first, n, k_rows, nc.vector)
+            first += n

@@ -62,7 +62,7 @@ def tile_mha_pa_t_kernel(
         const = stack.enter_context(tc.tile_pool(name="const", bufs=1))
         stage = stack.enter_context(tc.tile_pool(name="stage", bufs=4))
         terms = stack.enter_context(tc.tile_pool(name="terms", bufs=3))
-        results = stack.enter_context(tc.tile_pool(name="results", bufs=6))
+        results = stack.enter_context(tc.tile_pool(name="results", bufs=8))
         xt_pool = stack.enter_context(tc.psum_pool(name="xt", bufs=PSUM_SLOTS))
         qkv_pool = stack.enter_context(tc.psum_pool(name="qkv", bufs=PSUM_SLOTS))
         stack.enter_context(tc.manual_schedule())

@@ -21,6 +21,7 @@ Q_COLS, K_COLS, V_COLS = 128, 64, 64
 QKV_COLS = Q_COLS + K_COLS + V_COLS
 ROT_COLS = Q_COLS + K_COLS
 HEADS = 3
+Q_HEADS = 2
 PAIRS = 32
 ROT_PAIRS = HEADS * PAIRS
 Q_PAIRS = Q_COLS // 2
@@ -70,9 +71,11 @@ def tile_mha_pa_t_kernel(
         identity = const.tile([P, P], F32, name="identity")
         make_identity(nc, identity[:])
 
+        w_words_in = const.tile([P, 2 * QKV_COLS], U8, name="w_words_in", align_bytes=64)
+        w_scales_in = const.tile([P, QKV_COLS], U8, name="w_scales_in", align_bytes=64)
         w_words = const.tile([P, 2 * QKV_COLS], U8, name="w_words", align_bytes=64)
         w_scales = const.tile([P, QKV_COLS], U8, name="w_scales", align_bytes=64)
-        nc.vector.memset(w_scales[:].bitcast(I32), 0)
+        nc.vector.memset(w_scales_in[:].bitcast(I32), 0)
 
         head_tiles = sum(CHUNK_BANKS[:HEAD_CHUNKS]) * BANK_TILES
         table_head = const.tile([P, 4, head_tiles, PAIRS], BF16, name="table_head")
@@ -93,10 +96,10 @@ def tile_mha_pa_t_kernel(
             nc.sync.dma_start(out=x_chunks[c][:], in_=x_rows[:, tiles_of(c), :])
 
         load_x(0)
-        nc.sync.dma_start(out=w_words[:].bitcast(I32), in_=wqkv_words[0].bitcast(I32))
+        nc.sync.dma_start(out=w_words_in[:].bitcast(I32), in_=wqkv_words[0].bitcast(I32))
         for r in range(4):
             nc.sync.dma_start(
-                out=w_scales[r:P:32, :].bitcast(I32), in_=wqkv_scales[0, r:16:4, :].bitcast(I32)
+                out=w_scales_in[r:P:32, :].bitcast(I32), in_=wqkv_scales[0, r:16:4, :].bitcast(I32)
             )
         for c in range(1, 3):
             load_x(c)
@@ -108,6 +111,20 @@ def tile_mha_pa_t_kernel(
         nc.sync.dma_start(out=table_rest[:, 1], in_=sin_rows[:, head_tiles:TILES, :])
         for c in range(6, CHUNKS):
             load_x(c)
+
+        nc.vector.tensor_copy(
+            out=w_words[:].bitcast(I32)[:, 0:ROT_PAIRS].rearrange("p (i h) -> p h i", h=HEADS),
+            in_=w_words_in[:].bitcast(I32)[:, 0:ROT_PAIRS].rearrange("p (h i) -> p h i", h=HEADS),
+        )
+        nc.vector.tensor_copy(
+            out=w_words[:].bitcast(I32)[:, ROT_PAIRS : QKV_COLS // 2],
+            in_=w_words_in[:].bitcast(I32)[:, ROT_PAIRS : QKV_COLS // 2],
+        )
+        nc.vector.tensor_copy(
+            out=w_scales[:, 0:ROT_COLS].rearrange("p (i h e) -> p h i e", h=HEADS, e=2),
+            in_=w_scales_in[:, 0:ROT_COLS].rearrange("p (h i e) -> p h i e", h=HEADS, e=2),
+        )
+        nc.vector.tensor_copy(out=w_scales[:, ROT_COLS:QKV_COLS], in_=w_scales_in[:, ROT_COLS:QKV_COLS])
 
         grouped_of = {}
         codes_of = {}
@@ -176,24 +193,23 @@ def tile_mha_pa_t_kernel(
                 project_bank(done["projected"])
                 done["projected"] += 1
 
-        def multiply_bank(b, shares):
+        def multiply_bank(b, e):
             c = chunk_of[b]
-            for j in range(BANK_TILES):
-                at = (b - first_bank[c]) * BANK_TILES + j
-                for e in range(2):
-                    nc.vector.tensor_tensor(
-                        out=shares[:, at, e].rearrange("p (h i) r -> p h i r", h=HEADS),
-                        in0=qkv_of[b][:, j, 0:ROT_COLS]
-                        .rearrange("p (h i e) -> p h i e", h=HEADS, e=2)[:, :, :, e]
-                        .unsqueeze(3)
-                        .to_broadcast([P, HEADS, PAIRS, 2]),
-                        in1=factors_of(c)[:, 2 * e : 2 * e + 2, at, :]
-                        .rearrange("p r i -> p i r")
-                        .unsqueeze(1)
-                        .to_broadcast([P, HEADS, PAIRS, 2]),
-                        op=MULT,
-                    )
-            done["multiplied"] = b + 1
+            at = (b - first_bank[c]) * BANK_TILES
+            nc.vector.tensor_tensor(
+                out=shares_of[c][:, e, :, at : at + BANK_TILES, :, :].rearrange("p h j i r -> p j i h r"),
+                in0=qkv_of[b][:, :, 0:ROT_COLS]
+                .rearrange("p j (i h e) -> p j i h e", h=HEADS, e=2)[:, :, :, :, e]
+                .unsqueeze(4)
+                .to_broadcast([P, BANK_TILES, PAIRS, HEADS, 2]),
+                in1=factors_of(c)[:, 2 * e : 2 * e + 2, at : at + BANK_TILES, :]
+                .rearrange("p r j i -> p j i r")
+                .unsqueeze(3)
+                .to_broadcast([P, BANK_TILES, PAIRS, HEADS, 2]),
+                op=MULT,
+            )
+            if e == 1:
+                done["multiplied"] = b + 1
 
         def store_v(c):
             n = CHUNK_BANKS[c] * BANK_TILES
@@ -203,14 +219,14 @@ def tile_mha_pa_t_kernel(
             tiles = slice(first_bank[c] * BANK_TILES + first, first_bank[c] * BANK_TILES + first + n)
             if out_rows is q_rows:
                 out_sb = results.tile([P, MAX_TILES, Q_COLS], F32, name="q_sb")
-                pairs = slice(0, Q_PAIRS)
+                heads = slice(0, Q_HEADS)
             else:
                 out_sb = results.tile([P, MAX_TILES, K_COLS], F32, name="k_sb")
-                pairs = slice(Q_PAIRS, ROT_PAIRS)
+                heads = slice(Q_HEADS, HEADS)
             adder.tensor_tensor(
-                out=out_sb[:, 0:n, :].rearrange("p t (n r) -> p t n r", r=2),
-                in0=shares_of[c][:, first : first + n, 0, pairs, :],
-                in1=shares_of[c][:, first : first + n, 1, pairs, :],
+                out=out_sb[:, 0:n, :].rearrange("p t (h i r) -> p h t i r", i=PAIRS, r=2),
+                in0=shares_of[c][:, 0, heads, first : first + n, :, :],
+                in1=shares_of[c][:, 1, heads, first : first + n, :, :],
                 op=ADD,
             )
             nc.sync.dma_start(out=out_rows[:, tiles, :], in_=out_sb[:, 0:n, :])
@@ -226,11 +242,12 @@ def tile_mha_pa_t_kernel(
             project_what_fits()
             if c + LEAD < CHUNKS:
                 transpose_chunk(c + LEAD)
-            shares = terms.tile([P, MAX_TILES, 2, ROT_PAIRS, 2], F32, name="shares")
-            shares_of[c] = shares
-            for b in range(first_bank[c], first_bank[c] + CHUNK_BANKS[c]):
-                multiply_bank(b, shares)
-                if (b + 1 - first_bank[c]) % RUN_BANKS == 0 or b + 1 == first_bank[c] + CHUNK_BANKS[c]:
+            shares_of[c] = terms.tile([P, 2, HEADS, MAX_TILES, PAIRS, 2], F32, name="shares")
+            last = first_bank[c] + CHUNK_BANKS[c] - 1
+            for b in range(first_bank[c], last + 1):
+                multiply_bank(b, 0)
+                multiply_bank(b, 1)
+                if (b + 1 - first_bank[c]) % RUN_BANKS == 0 or b == last:
                     project_what_fits()
             store_v(c)
             n = CHUNK_BANKS[c] * BANK_TILES

@@ -34,6 +34,7 @@ CHUNK_BANKS = (1, 1, 2, 2, 2, 4, 4, 4, 4, 4, 4)
 HEAD_CHUNKS = 5
 CHUNKS = len(CHUNK_BANKS)
 MAX_TILES = max(CHUNK_BANKS) * BANK_TILES
+LATE = 8
 RUN_BANKS = 2
 LEAD = 3
 TAIL_UNITS = (5, 3)
@@ -63,7 +64,7 @@ def tile_mha_pa_t_kernel(
         const = stack.enter_context(tc.tile_pool(name="const", bufs=1))
         stage = stack.enter_context(tc.tile_pool(name="stage", bufs=4))
         terms = stack.enter_context(tc.tile_pool(name="terms", bufs=3))
-        results = stack.enter_context(tc.tile_pool(name="results", bufs=8))
+        results = stack.enter_context(tc.tile_pool(name="results", bufs=7))
         xt_pool = stack.enter_context(tc.psum_pool(name="xt", bufs=PSUM_SLOTS))
         qkv_pool = stack.enter_context(tc.psum_pool(name="qkv", bufs=PSUM_SLOTS))
         stack.enter_context(tc.manual_schedule())
@@ -126,19 +127,70 @@ def tile_mha_pa_t_kernel(
         )
         nc.vector.tensor_copy(out=w_scales[:, ROT_COLS:QKV_COLS], in_=w_scales_in[:, ROT_COLS:QKV_COLS])
 
+        w_parity = const.tile([P, 2, 2 * P], U8, name="w_parity", align_bytes=64)
+        w_parity_scales = const.tile([P, 2, P], U8, name="w_parity_scales", align_bytes=64)
+
+        def split_w_by_parity():
+            nc.vector.tensor_copy(
+                out=w_parity[:, :, 0 : 2 * ROT_PAIRS].rearrange("p e (n b) -> p e n b", b=2),
+                in_=w_words_in[:, 0 : 2 * ROT_COLS].rearrange("p (n e b) -> p e n b", e=2, b=2),
+            )
+            nc.vector.tensor_copy(
+                out=w_parity[:, :, 2 * ROT_PAIRS : 2 * P],
+                in_=w_words_in[:, 2 * ROT_COLS : 2 * QKV_COLS].rearrange("p (e n) -> p e n", e=2),
+            )
+            nc.vector.tensor_copy(
+                out=w_parity_scales[:, :, 0:ROT_PAIRS],
+                in_=w_scales_in[:, 0:ROT_COLS].rearrange("p (n e) -> p e n", e=2),
+            )
+            nc.vector.tensor_copy(
+                out=w_parity_scales[:, :, ROT_PAIRS:P],
+                in_=w_scales_in[:, ROT_COLS:QKV_COLS].rearrange("p (e n) -> p e n", e=2),
+            )
+
+        late_tile = first_bank[LATE] * BANK_TILES
+        late_table = const.tile([P, 2, TILES - late_tile, PAIRS], F32, name="late_table")
+        plus = const.tile([P, P], BF16, name="plus")
+        minus = const.tile([P, P], BF16, name="minus")
+        nc.scalar.copy(out=plus[:], in_=identity[:])
+        nc.scalar.mul(out=minus[:], in_=identity[:], mul=-1.0)
+
+        def make_late_table(c):
+            tiles = tiles_of(c)
+            n = tiles.stop - tiles.start
+            for r in range(2):
+                total = xt_pool.tile([P, BANK_TILES, 2, P], F32, name="xt")
+                columns = total[:].rearrange("p j half r -> p (j half r)")[:, 0 : n * PAIRS]
+                for factor, sign in ((1, (minus, plus)[r]), (0, minus)):
+                    nc.tensor.matmul(
+                        out=columns,
+                        lhsT=sign[:],
+                        rhs=factors_of(c)[:, factor].rearrange("p t i -> p (t i)"),
+                        start=factor == 1,
+                        stop=factor == 0,
+                    )
+                nc.scalar.copy(
+                    out=late_table[:, r, tiles.start - late_tile : tiles.stop - late_tile, :].rearrange(
+                        "p t i -> p (t i)"
+                    ),
+                    in_=columns,
+                )
+
         grouped_of = {}
         codes_of = {}
         scales_of = {}
         qkv_of = {}
+        sums_of = {}
         v_of = {}
         shares_of = {}
         done = {"quantized": 0, "projected": 0, "multiplied": 0}
         bank_words = BANK_TILES * K_WORDS
 
-        def transpose_chunk(c):
-            grouped_of[c] = stage.tile([P, MAX_TILES * K], BF16, name="grouped", align_bytes=64)
+        def transpose_banks(c, first, stop):
+            if first == 0:
+                grouped_of[c] = stage.tile([P, MAX_TILES * K], BF16, name="grouped", align_bytes=64)
             words = x_chunks[c][:].bitcast(F32)
-            for b in range(CHUNK_BANKS[c]):
+            for b in range(first, stop):
                 xt = xt_pool.tile([P, BANK_TILES, 2, P], F32, name="xt")
                 for j in range(BANK_TILES):
                     for half in range(2):
@@ -154,6 +206,9 @@ def tile_mha_pa_t_kernel(
                     in_=xt[:].rearrange("p j half r -> p j r half"),
                 )
 
+        def transpose_chunk(c):
+            transpose_banks(c, 0, CHUNK_BANKS[c])
+
         def quantize_chunk(c):
             columns = CHUNK_BANKS[c] * BANK_TILES * P
             codes_of[c] = stage.tile([P, MAX_TILES * P], U32, name="codes", align_bytes=64)
@@ -164,9 +219,10 @@ def tile_mha_pa_t_kernel(
                 in_=grouped_of[c][:, 0 : 4 * columns],
             )
             done["quantized"] = first_bank[c] + CHUNK_BANKS[c]
-            factors = factors_of(c)
-            nc.scalar.mul(out=factors[:, 2], in_=factors[:, 1], mul=-1.0)
-            nc.scalar.copy(out=factors[:, 3], in_=factors[:, 0])
+            if c < LATE:
+                factors = factors_of(c)
+                nc.scalar.mul(out=factors[:, 2], in_=factors[:, 1], mul=-1.0)
+                nc.scalar.copy(out=factors[:, 3], in_=factors[:, 0])
 
         def project_bank(b):
             c = chunk_of[b]
@@ -186,6 +242,20 @@ def tile_mha_pa_t_kernel(
                     start=True,
                     stop=True,
                 )
+            if c >= LATE:
+                sums_of[b] = xt_pool.tile([P, BANK_TILES, 2, P], F32, name="xt")
+                for j in range(BANK_TILES):
+                    rows = slice((at + j) * P, (at + j + 1) * P)
+                    for e in range(2):
+                        nc.tensor.matmul_mx(
+                            out=sums_of[b][:, j, 0, :],
+                            lhsT=codes_of[c][:, rows].bitcast(FP8X4),
+                            lhsT_scale=scales_of[c][:, rows],
+                            rhs=w_parity[:, e, :].bitcast(FP4X4),
+                            rhs_scale=w_parity_scales[:, e, :],
+                            start=e == 0,
+                            stop=e == 1,
+                        )
             nc.scalar.copy(out=v_of[c][:, at : at + BANK_TILES, :], in_=qkv[:, :, ROT_COLS:QKV_COLS])
 
         def project_what_fits():
@@ -211,6 +281,38 @@ def tile_mha_pa_t_kernel(
             if e == 1:
                 done["multiplied"] = b + 1
 
+        def common_of(c):
+            return (
+                shares_of[c][:, 0]
+                .rearrange("p h t i r -> p (h t i r)")[:, 0 : MAX_TILES * ROT_PAIRS]
+                .rearrange("p (h t i) -> p h t i", h=HEADS, t=MAX_TILES)
+            )
+
+        def multiply_late_bank(b):
+            c = chunk_of[b]
+            at = (b - first_bank[c]) * BANK_TILES
+            tile = b * BANK_TILES
+            nc.vector.tensor_tensor(
+                out=shares_of[c][:, 1, :, at : at + BANK_TILES, :, :].rearrange("p h j i r -> p j i h r"),
+                in0=qkv_of[b][:, :, 0:ROT_COLS].rearrange("p j (i h e) -> p j i h e", h=HEADS, e=2)[
+                    :, :, :, :, ::-1
+                ],
+                in1=late_table[:, :, tile - late_tile : tile - late_tile + BANK_TILES, :]
+                .rearrange("p r j i -> p j i r")
+                .unsqueeze(3)
+                .to_broadcast([P, BANK_TILES, PAIRS, HEADS, 2]),
+                op=MULT,
+            )
+            nc.vector.tensor_tensor(
+                out=common_of(c)[:, :, at : at + BANK_TILES, :].rearrange("p h j i -> p j h i"),
+                in0=sums_of[b][:, :, 0, 0:ROT_PAIRS].rearrange("p j (h i) -> p j h i", h=HEADS),
+                in1=factors_of(c)[:, 0, at : at + BANK_TILES, :]
+                .unsqueeze(2)
+                .to_broadcast([P, BANK_TILES, HEADS, PAIRS]),
+                op=MULT,
+            )
+            done["multiplied"] = b + 1
+
         def store_v(c):
             n = CHUNK_BANKS[c] * BANK_TILES
             nc.sync.dma_start(out=v_rows[:, tiles_of(c), :], in_=v_of[c][:, 0:n, :])
@@ -225,7 +327,11 @@ def tile_mha_pa_t_kernel(
                 heads = slice(Q_HEADS, HEADS)
             adder.tensor_tensor(
                 out=out_sb[:, 0:n, :].rearrange("p t (h i r) -> p h t i r", i=PAIRS, r=2),
-                in0=shares_of[c][:, 0, heads, first : first + n, :, :],
+                in0=common_of(c)[:, heads, first : first + n, :]
+                .unsqueeze(4)
+                .to_broadcast([P, heads.stop - heads.start, n, PAIRS, 2])
+                if c >= LATE
+                else shares_of[c][:, 0, heads, first : first + n, :, :],
                 in1=shares_of[c][:, 1, heads, first : first + n, :, :],
                 op=ADD,
             )
@@ -240,15 +346,27 @@ def tile_mha_pa_t_kernel(
             if c + 1 < CHUNKS:
                 quantize_chunk(c + 1)
             project_what_fits()
-            if c + LEAD < CHUNKS:
+            if c <= LATE - 3:
                 transpose_chunk(c + LEAD)
+            elif c < LATE:
+                transpose_banks(c + LEAD, 2, CHUNK_BANKS[c + LEAD])
+                make_late_table(c + LEAD)
+            if c == 0:
+                split_w_by_parity()
             shares_of[c] = terms.tile([P, 2, HEADS, MAX_TILES, PAIRS, 2], F32, name="shares")
             last = first_bank[c] + CHUNK_BANKS[c] - 1
             for b in range(first_bank[c], last + 1):
-                multiply_bank(b, 0)
-                multiply_bank(b, 1)
+                if c >= LATE:
+                    multiply_late_bank(b)
+                else:
+                    multiply_bank(b, 0)
+                    multiply_bank(b, 1)
                 if (b + 1 - first_bank[c]) % RUN_BANKS == 0 or b == last:
                     project_what_fits()
+                    if LATE - 3 <= c < LATE - 1 and b < last:
+                        transpose_banks(c + LEAD + 1, 0, 2)
+            if c == LATE - 3:
+                make_late_table(LATE)
             store_v(c)
             n = CHUNK_BANKS[c] * BANK_TILES
             if c < CHUNKS - 1:

@@ -113,17 +113,22 @@ def tile_mha_pa_t_kernel(
         for c in range(6, CHUNKS):
             load_x(c)
 
-        nc.vector.tensor_copy(
-            out=w_words[:].bitcast(I32)[:, 0:ROT_PAIRS].rearrange("p (i h) -> p h i", h=HEADS),
-            in_=w_words_in[:].bitcast(I32)[:, 0:ROT_PAIRS].rearrange("p (h i) -> p h i", h=HEADS),
-        )
+        for e in range(2):
+            nc.vector.tensor_copy(
+                out=w_words[:, 0 : 2 * ROT_COLS].rearrange("p (i h o b) -> p h i o b", h=HEADS, o=2, b=2)[
+                    :, :, :, 1 - e, :
+                ],
+                in_=w_words_in[:, 0 : 2 * ROT_COLS].rearrange("p (h i e b) -> p h i e b", h=HEADS, e=2, b=2)[
+                    :, :, :, e, :
+                ],
+            )
+            nc.vector.tensor_copy(
+                out=w_scales[:, 0:ROT_COLS].rearrange("p (i h o) -> p h i o", h=HEADS, o=2)[:, :, :, 1 - e],
+                in_=w_scales_in[:, 0:ROT_COLS].rearrange("p (h i e) -> p h i e", h=HEADS, e=2)[:, :, :, e],
+            )
         nc.vector.tensor_copy(
             out=w_words[:].bitcast(I32)[:, ROT_PAIRS : QKV_COLS // 2],
             in_=w_words_in[:].bitcast(I32)[:, ROT_PAIRS : QKV_COLS // 2],
-        )
-        nc.vector.tensor_copy(
-            out=w_scales[:, 0:ROT_COLS].rearrange("p (i h e) -> p h i e", h=HEADS, e=2),
-            in_=w_scales_in[:, 0:ROT_COLS].rearrange("p (h i e) -> p h i e", h=HEADS, e=2),
         )
         nc.vector.tensor_copy(out=w_scales[:, ROT_COLS:QKV_COLS], in_=w_scales_in[:, ROT_COLS:QKV_COLS])
 
@@ -269,7 +274,7 @@ def tile_mha_pa_t_kernel(
             nc.vector.tensor_tensor(
                 out=shares_of[c][:, e, :, at : at + BANK_TILES, :, :].rearrange("p h j i r -> p j i h r"),
                 in0=qkv_of[b][:, :, 0:ROT_COLS]
-                .rearrange("p j (i h e) -> p j i h e", h=HEADS, e=2)[:, :, :, :, e]
+                .rearrange("p j (i h o) -> p j i h o", h=HEADS, o=2)[:, :, :, :, 1 - e]
                 .unsqueeze(4)
                 .to_broadcast([P, BANK_TILES, PAIRS, HEADS, 2]),
                 in1=factors_of(c)[:, 2 * e : 2 * e + 2, at : at + BANK_TILES, :]
@@ -294,9 +299,7 @@ def tile_mha_pa_t_kernel(
             tile = b * BANK_TILES
             nc.vector.tensor_tensor(
                 out=shares_of[c][:, 1, :, at : at + BANK_TILES, :, :].rearrange("p h j i r -> p j i h r"),
-                in0=qkv_of[b][:, :, 0:ROT_COLS].rearrange("p j (i h e) -> p j i h e", h=HEADS, e=2)[
-                    :, :, :, :, ::-1
-                ],
+                in0=qkv_of[b][:, :, 0:ROT_COLS].rearrange("p j (i h o) -> p j i h o", h=HEADS, o=2),
                 in1=late_table[:, :, tile - late_tile : tile - late_tile + BANK_TILES, :]
                 .rearrange("p r j i -> p j i r")
                 .unsqueeze(3)
@@ -304,11 +307,11 @@ def tile_mha_pa_t_kernel(
                 op=MULT,
             )
             nc.vector.tensor_tensor(
-                out=common_of(c)[:, :, at : at + BANK_TILES, :].rearrange("p h j i -> p j h i"),
-                in0=sums_of[b][:, :, 0, 0:ROT_PAIRS].rearrange("p j (h i) -> p j h i", h=HEADS),
+                out=common_of(c)[:, :, at : at + BANK_TILES, :],
+                in0=sums_of[b][:, :, 0, 0:ROT_PAIRS].rearrange("p j (h i) -> p h j i", h=HEADS),
                 in1=factors_of(c)[:, 0, at : at + BANK_TILES, :]
-                .unsqueeze(2)
-                .to_broadcast([P, BANK_TILES, HEADS, PAIRS]),
+                .unsqueeze(1)
+                .to_broadcast([P, HEADS, BANK_TILES, PAIRS]),
                 op=MULT,
             )
             done["multiplied"] = b + 1

@@ -37,7 +37,8 @@ MAX_TILES = max(CHUNK_BANKS) * BANK_TILES
 LATE = 8
 RUN_BANKS = 2
 LEAD = 3
-TAIL_UNITS = (5, 3)
+PENULTIMATE_UNITS = (4, 4)
+LAST_UNITS = (5, 3)
 
 FLOPS = 2 * ROWS * K * QKV_COLS
 
@@ -262,6 +263,8 @@ def tile_mha_pa_t_kernel(
                             stop=e == 1,
                         )
             nc.scalar.copy(out=v_of[c][:, at : at + BANK_TILES, :], in_=qkv[:, :, ROT_COLS:QKV_COLS])
+            if b + 1 == first_bank[c] + CHUNK_BANKS[c]:
+                nc.sync.dma_start(out=v_rows[:, tiles_of(c), :], in_=v_of[c][:, 0 : CHUNK_BANKS[c] * BANK_TILES, :])
 
         def project_what_fits():
             while done["projected"] < min(done["quantized"], done["multiplied"] + PSUM_SLOTS):
@@ -316,10 +319,6 @@ def tile_mha_pa_t_kernel(
             )
             done["multiplied"] = b + 1
 
-        def store_v(c):
-            n = CHUNK_BANKS[c] * BANK_TILES
-            nc.sync.dma_start(out=v_rows[:, tiles_of(c), :], in_=v_of[c][:, 0:n, :])
-
         def add_and_store(c, first, n, out_rows, adder):
             tiles = slice(first_bank[c] * BANK_TILES + first, first_bank[c] * BANK_TILES + first + n)
             if out_rows is q_rows:
@@ -370,15 +369,13 @@ def tile_mha_pa_t_kernel(
                         transpose_banks(c + LEAD + 1, 0, 2)
             if c == LATE - 3:
                 make_late_table(LATE)
-            store_v(c)
-            n = CHUNK_BANKS[c] * BANK_TILES
-            if c < CHUNKS - 1:
-                add_and_store(c, 0, n, q_rows, nc.gpsimd)
             if c < CHUNKS - 2:
+                n = CHUNK_BANKS[c] * BANK_TILES
+                add_and_store(c, 0, n, q_rows, nc.gpsimd)
                 add_and_store(c, 0, n, k_rows, nc.gpsimd)
-        add_and_store(CHUNKS - 2, 0, CHUNK_BANKS[CHUNKS - 2] * BANK_TILES, k_rows, nc.vector)
-        first = 0
-        for n in TAIL_UNITS:
-            add_and_store(CHUNKS - 1, first, n, q_rows, nc.vector)
-            add_and_store(CHUNKS - 1, first, n, k_rows, nc.vector)
-            first += n
+        for c, units in ((CHUNKS - 2, PENULTIMATE_UNITS), (CHUNKS - 1, LAST_UNITS)):
+            first = 0
+            for n in units:
+                add_and_store(c, first, n, q_rows, nc.vector)
+                add_and_store(c, first, n, k_rows, nc.vector)
+                first += n

from contextlib import ExitStack

import concourse.mybir as mybir
from concourse.masks import make_identity

F32 = mybir.dt.float32
BF16 = mybir.dt.bfloat16
I32 = mybir.dt.int32
U32 = mybir.dt.uint32
U8 = mybir.dt.uint8
FP8X4 = mybir.dt.float8_e4m3fn_x4
FP4X4 = mybir.dt.float4_e2m1fn_x4
MULT = mybir.AluOpType.mult
ADD = mybir.AluOpType.add

P = 128
ROWS = 8192
K = 512
K_WORDS = K // 2
Q_COLS, K_COLS, V_COLS = 128, 64, 64
QKV_COLS = Q_COLS + K_COLS + V_COLS
ROT_COLS = Q_COLS + K_COLS
HEADS = 3
Q_HEADS = 2
PAIRS = 32
ROT_PAIRS = HEADS * PAIRS
Q_PAIRS = Q_COLS // 2

TILES = ROWS // P
BANK_TILES = 2
BANKS = TILES // BANK_TILES
PSUM_SLOTS = 4
CHUNK_BANKS = (1, 1, 2, 2, 2, 4, 4, 4, 4, 4, 4)
HEAD_CHUNKS = 5
CHUNKS = len(CHUNK_BANKS)
MAX_TILES = max(CHUNK_BANKS) * BANK_TILES
LATE = 8
RUN_BANKS = 2
LEAD = 3
PENULTIMATE_UNITS = (4, 4)
LAST_UNITS = (5, 3)

FLOPS = 2 * ROWS * K * QKV_COLS


def tile_mha_pa_t_kernel(
    tc, x, freqs_cos, freqs_sin, wqkv_words, wqkv_scales, out_0, out_1, out_2
):
    nc = tc.nc
    x_rows = x.rearrange("(p t) k -> p t k", t=TILES)
    cos_rows = freqs_cos.rearrange("(p t) i -> p t i", t=TILES)
    sin_rows = freqs_sin.rearrange("(p t) i -> p t i", t=TILES)
    q_rows = out_0.rearrange("(p t) h d -> p t (h d)", t=TILES)
    k_rows = out_1.rearrange("(p t) h d -> p t (h d)", t=TILES)
    v_rows = out_2.rearrange("(p t) h d -> p t (h d)", t=TILES)

    assert sum(CHUNK_BANKS) == BANKS
    first_bank = [sum(CHUNK_BANKS[:c]) for c in range(CHUNKS)]
    chunk_of = [c for c in range(CHUNKS) for b in range(CHUNK_BANKS[c])]

    def tiles_of(c):
        return slice(first_bank[c] * BANK_TILES, (first_bank[c] + CHUNK_BANKS[c]) * BANK_TILES)

    with ExitStack() as stack:
        const = stack.enter_context(tc.tile_pool(name="const", bufs=1))
        stage = stack.enter_context(tc.tile_pool(name="stage", bufs=4))
        terms = stack.enter_context(tc.tile_pool(name="terms", bufs=3))
        results = stack.enter_context(tc.tile_pool(name="results", bufs=7))
        xt_pool = stack.enter_context(tc.psum_pool(name="xt", bufs=PSUM_SLOTS))
        qkv_pool = stack.enter_context(tc.psum_pool(name="qkv", bufs=PSUM_SLOTS))
        stack.enter_context(tc.manual_schedule())

        identity = const.tile([P, P], F32, name="identity")
        make_identity(nc, identity[:])

        w_words_in = const.tile([P, 2 * QKV_COLS], U8, name="w_words_in", align_bytes=64)
        w_scales_in = const.tile([P, QKV_COLS], U8, name="w_scales_in", align_bytes=64)
        w_words = const.tile([P, 2 * QKV_COLS], U8, name="w_words", align_bytes=64)
        w_scales = const.tile([P, QKV_COLS], U8, name="w_scales", align_bytes=64)
        nc.vector.memset(w_scales_in[:].bitcast(I32), 0)

        head_tiles = sum(CHUNK_BANKS[:HEAD_CHUNKS]) * BANK_TILES
        table_head = const.tile([P, 4, head_tiles, PAIRS], BF16, name="table_head")
        table_rest = const.tile([P, 4, TILES - head_tiles, PAIRS], BF16, name="table_rest")

        def factors_of(c):
            tiles = tiles_of(c)
            if c < HEAD_CHUNKS:
                return table_head[:, :, tiles, :]
            return table_rest[:, :, tiles.start - head_tiles : tiles.stop - head_tiles, :]

        x_chunks = []
        for c in range(CHUNKS):
            x_chunk = const.tile([P, CHUNK_BANKS[c] * BANK_TILES, K], BF16, name="x_chunk%d" % c)
            x_chunks.append(x_chunk)

        def load_x(c):
            nc.sync.dma_start(out=x_chunks[c][:], in_=x_rows[:, tiles_of(c), :])

        load_x(0)
        nc.sync.dma_start(out=w_words_in[:].bitcast(I32), in_=wqkv_words[0].bitcast(I32))
        for r in range(4):
            nc.sync.dma_start(
                out=w_scales_in[r:P:32, :].bitcast(I32), in_=wqkv_scales[0, r:16:4, :].bitcast(I32)
            )
        for c in range(1, 3):
            load_x(c)
        nc.sync.dma_start(out=table_head[:, 0], in_=cos_rows[:, 0:head_tiles, :])
        nc.sync.dma_start(out=table_head[:, 1], in_=sin_rows[:, 0:head_tiles, :])
        for c in range(3, 6):
            load_x(c)
        nc.sync.dma_start(out=table_rest[:, 0], in_=cos_rows[:, head_tiles:TILES, :])
        nc.sync.dma_start(out=table_rest[:, 1], in_=sin_rows[:, head_tiles:TILES, :])
        for c in range(6, CHUNKS):
            load_x(c)

        for e in range(2):
            nc.vector.tensor_copy(
                out=w_words[:, 0 : 2 * ROT_COLS].rearrange("p (i h o b) -> p h i o b", h=HEADS, o=2, b=2)[
                    :, :, :, 1 - e, :
                ],
                in_=w_words_in[:, 0 : 2 * ROT_COLS].rearrange("p (h i e b) -> p h i e b", h=HEADS, e=2, b=2)[
                    :, :, :, e, :
                ],
            )
            nc.vector.tensor_copy(
                out=w_scales[:, 0:ROT_COLS].rearrange("p (i h o) -> p h i o", h=HEADS, o=2)[:, :, :, 1 - e],
                in_=w_scales_in[:, 0:ROT_COLS].rearrange("p (h i e) -> p h i e", h=HEADS, e=2)[:, :, :, e],
            )
        nc.vector.tensor_copy(
            out=w_words[:].bitcast(I32)[:, ROT_PAIRS : QKV_COLS // 2],
            in_=w_words_in[:].bitcast(I32)[:, ROT_PAIRS : QKV_COLS // 2],
        )
        nc.vector.tensor_copy(out=w_scales[:, ROT_COLS:QKV_COLS], in_=w_scales_in[:, ROT_COLS:QKV_COLS])

        w_parity = const.tile([P, 2, 2 * P], U8, name="w_parity", align_bytes=64)
        w_parity_scales = const.tile([P, 2, P], U8, name="w_parity_scales", align_bytes=64)

        def split_w_by_parity():
            nc.vector.tensor_copy(
                out=w_parity[:, :, 0 : 2 * ROT_PAIRS].rearrange("p e (n b) -> p e n b", b=2),
                in_=w_words_in[:, 0 : 2 * ROT_COLS].rearrange("p (n e b) -> p e n b", e=2, b=2),
            )
            nc.vector.tensor_copy(
                out=w_parity[:, :, 2 * ROT_PAIRS : 2 * P],
                in_=w_words_in[:, 2 * ROT_COLS : 2 * QKV_COLS].rearrange("p (e n) -> p e n", e=2),
            )
            nc.vector.tensor_copy(
                out=w_parity_scales[:, :, 0:ROT_PAIRS],
                in_=w_scales_in[:, 0:ROT_COLS].rearrange("p (n e) -> p e n", e=2),
            )
            nc.vector.tensor_copy(
                out=w_parity_scales[:, :, ROT_PAIRS:P],
                in_=w_scales_in[:, ROT_COLS:QKV_COLS].rearrange("p (e n) -> p e n", e=2),
            )

        late_tile = first_bank[LATE] * BANK_TILES
        late_table = const.tile([P, 2, TILES - late_tile, PAIRS], F32, name="late_table")
        plus = const.tile([P, P], BF16, name="plus")
        minus = const.tile([P, P], BF16, name="minus")
        nc.scalar.copy(out=plus[:], in_=identity[:])
        nc.scalar.mul(out=minus[:], in_=identity[:], mul=-1.0)

        def make_late_table(c):
            tiles = tiles_of(c)
            n = tiles.stop - tiles.start
            for r in range(2):
                total = xt_pool.tile([P, BANK_TILES, 2, P], F32, name="xt")
                columns = total[:].rearrange("p j half r -> p (j half r)")[:, 0 : n * PAIRS]
                for factor, sign in ((1, (minus, plus)[r]), (0, minus)):
                    nc.tensor.matmul(
                        out=columns,
                        lhsT=sign[:],
                        rhs=factors_of(c)[:, factor].rearrange("p t i -> p (t i)"),
                        start=factor == 1,
                        stop=factor == 0,
                    )
                nc.scalar.copy(
                    out=late_table[:, r, tiles.start - late_tile : tiles.stop - late_tile, :].rearrange(
                        "p t i -> p (t i)"
                    ),
                    in_=columns,
                )

        grouped_of = {}
        codes_of = {}
        scales_of = {}
        qkv_of = {}
        sums_of = {}
        v_of = {}
        shares_of = {}
        done = {"quantized": 0, "projected": 0, "multiplied": 0}
        bank_words = BANK_TILES * K_WORDS

        def transpose_banks(c, first, stop):
            if first == 0:
                grouped_of[c] = stage.tile([P, MAX_TILES * K], BF16, name="grouped", align_bytes=64)
            words = x_chunks[c][:].bitcast(F32)
            for b in range(first, stop):
                xt = xt_pool.tile([P, BANK_TILES, 2, P], F32, name="xt")
                for j in range(BANK_TILES):
                    for half in range(2):
                        nc.tensor.transpose(
                            out=xt[:, j, half, :],
                            in_=words[:, b * BANK_TILES + j, half:K_WORDS:2],
                            identity=identity[:],
                        )
                nc.scalar.copy(
                    out=grouped_of[c][:]
                    .bitcast(F32)[:, b * bank_words : (b + 1) * bank_words]
                    .rearrange("p (j r half) -> p j r half", j=BANK_TILES, half=2),
                    in_=xt[:].rearrange("p j half r -> p j r half"),
                )

        def transpose_chunk(c):
            transpose_banks(c, 0, CHUNK_BANKS[c])

        def quantize_chunk(c):
            columns = CHUNK_BANKS[c] * BANK_TILES * P
            codes_of[c] = stage.tile([P, MAX_TILES * P], U32, name="codes", align_bytes=64)
            scales_of[c] = stage.tile([P, MAX_TILES * P], U8, name="scales", align_bytes=64)
            nc.vector.quantize_mx(
                out=codes_of[c][:, 0:columns].bitcast(FP8X4),
                scales=scales_of[c][:, 0:columns],
                in_=grouped_of[c][:, 0 : 4 * columns],
            )
            done["quantized"] = first_bank[c] + CHUNK_BANKS[c]
            if c < LATE:
                factors = factors_of(c)
                nc.scalar.mul(out=factors[:, 2], in_=factors[:, 1], mul=-1.0)
                nc.scalar.copy(out=factors[:, 3], in_=factors[:, 0])

        def project_bank(b):
            c = chunk_of[b]
            if b == first_bank[c]:
                v_of[c] = results.tile([P, MAX_TILES, V_COLS], F32, name="v_sb")
            qkv = qkv_pool.tile([P, BANK_TILES, QKV_COLS], F32, name="qkv")
            qkv_of[b] = qkv
            at = (b - first_bank[c]) * BANK_TILES
            for j in range(BANK_TILES):
                rows = slice((at + j) * P, (at + j + 1) * P)
                nc.tensor.matmul_mx(
                    out=qkv[:, j, :],
                    lhsT=codes_of[c][:, rows].bitcast(FP8X4),
                    lhsT_scale=scales_of[c][:, rows],
                    rhs=w_words[:].bitcast(FP4X4),
                    rhs_scale=w_scales[:],
                    start=True,
                    stop=True,
                )
            if c >= LATE:
                sums_of[b] = xt_pool.tile([P, BANK_TILES, 2, P], F32, name="xt")
                for j in range(BANK_TILES):
                    rows = slice((at + j) * P, (at + j + 1) * P)
                    for e in range(2):
                        nc.tensor.matmul_mx(
                            out=sums_of[b][:, j, 0, :],
                            lhsT=codes_of[c][:, rows].bitcast(FP8X4),
                            lhsT_scale=scales_of[c][:, rows],
                            rhs=w_parity[:, e, :].bitcast(FP4X4),
                            rhs_scale=w_parity_scales[:, e, :],
                            start=e == 0,
                            stop=e == 1,
                        )
            nc.scalar.copy(out=v_of[c][:, at : at + BANK_TILES, :], in_=qkv[:, :, ROT_COLS:QKV_COLS])
            if b + 1 == first_bank[c] + CHUNK_BANKS[c]:
                nc.sync.dma_start(out=v_rows[:, tiles_of(c), :], in_=v_of[c][:, 0 : CHUNK_BANKS[c] * BANK_TILES, :])

        def project_what_fits():
            while done["projected"] < min(done["quantized"], done["multiplied"] + PSUM_SLOTS):
                project_bank(done["projected"])
                done["projected"] += 1

        def multiply_bank(b, e):
            c = chunk_of[b]
            at = (b - first_bank[c]) * BANK_TILES
            nc.vector.tensor_tensor(
                out=shares_of[c][:, e, :, at : at + BANK_TILES, :, :].rearrange("p h j i r -> p j i h r"),
                in0=qkv_of[b][:, :, 0:ROT_COLS]
                .rearrange("p j (i h o) -> p j i h o", h=HEADS, o=2)[:, :, :, :, 1 - e]
                .unsqueeze(4)
                .to_broadcast([P, BANK_TILES, PAIRS, HEADS, 2]),
                in1=factors_of(c)[:, 2 * e : 2 * e + 2, at : at + BANK_TILES, :]
                .rearrange("p r j i -> p j i r")
                .unsqueeze(3)
                .to_broadcast([P, BANK_TILES, PAIRS, HEADS, 2]),
                op=MULT,
            )
            if e == 1:
                done["multiplied"] = b + 1

        def common_of(c):
            return (
                shares_of[c][:, 0]
                .rearrange("p h t i r -> p (h t i r)")[:, 0 : MAX_TILES * ROT_PAIRS]
                .rearrange("p (h t i) -> p h t i", h=HEADS, t=MAX_TILES)
            )

        def multiply_late_bank(b):
            c = chunk_of[b]
            at = (b - first_bank[c]) * BANK_TILES
            tile = b * BANK_TILES
            nc.vector.tensor_tensor(
                out=shares_of[c][:, 1, :, at : at + BANK_TILES, :, :].rearrange("p h j i r -> p j i h r"),
                in0=qkv_of[b][:, :, 0:ROT_COLS].rearrange("p j (i h o) -> p j i h o", h=HEADS, o=2),
                in1=late_table[:, :, tile - late_tile : tile - late_tile + BANK_TILES, :]
                .rearrange("p r j i -> p j i r")
                .unsqueeze(3)
                .to_broadcast([P, BANK_TILES, PAIRS, HEADS, 2]),
                op=MULT,
            )
            nc.vector.tensor_tensor(
                out=common_of(c)[:, :, at : at + BANK_TILES, :],
                in0=sums_of[b][:, :, 0, 0:ROT_PAIRS].rearrange("p j (h i) -> p h j i", h=HEADS),
                in1=factors_of(c)[:, 0, at : at + BANK_TILES, :]
                .unsqueeze(1)
                .to_broadcast([P, HEADS, BANK_TILES, PAIRS]),
                op=MULT,
            )
            done["multiplied"] = b + 1

        def add_and_store(c, first, n, out_rows, adder):
            tiles = slice(first_bank[c] * BANK_TILES + first, first_bank[c] * BANK_TILES + first + n)
            if out_rows is q_rows:
                out_sb = results.tile([P, MAX_TILES, Q_COLS], F32, name="q_sb")
                heads = slice(0, Q_HEADS)
            else:
                out_sb = results.tile([P, MAX_TILES, K_COLS], F32, name="k_sb")
                heads = slice(Q_HEADS, HEADS)
            adder.tensor_tensor(
                out=out_sb[:, 0:n, :].rearrange("p t (h i r) -> p h t i r", i=PAIRS, r=2),
                in0=common_of(c)[:, heads, first : first + n, :]
                .unsqueeze(4)
                .to_broadcast([P, heads.stop - heads.start, n, PAIRS, 2])
                if c >= LATE
                else shares_of[c][:, 0, heads, first : first + n, :, :],
                in1=shares_of[c][:, 1, heads, first : first + n, :, :],
                op=ADD,
            )
            nc.sync.dma_start(out=out_rows[:, tiles, :], in_=out_sb[:, 0:n, :])

        transpose_chunk(0)
        transpose_chunk(1)
        quantize_chunk(0)
        project_what_fits()
        transpose_chunk(2)
        for c in range(CHUNKS):
            if c + 1 < CHUNKS:
                quantize_chunk(c + 1)
            project_what_fits()
            if c <= LATE - 3:
                transpose_chunk(c + LEAD)
            elif c < LATE:
                transpose_banks(c + LEAD, 2, CHUNK_BANKS[c + LEAD])
                make_late_table(c + LEAD)
            if c == 0:
                split_w_by_parity()
            shares_of[c] = terms.tile([P, 2, HEADS, MAX_TILES, PAIRS, 2], F32, name="shares")
            last = first_bank[c] + CHUNK_BANKS[c] - 1
            for b in range(first_bank[c], last + 1):
                if c >= LATE:
                    multiply_late_bank(b)
                else:
                    multiply_bank(b, 0)
                    multiply_bank(b, 1)
                if (b + 1 - first_bank[c]) % RUN_BANKS == 0 or b == last:
                    project_what_fits()
                    if LATE - 3 <= c < LATE - 1 and b < last:
                        transpose_banks(c + LEAD + 1, 0, 2)
            if c == LATE - 3:
                make_late_table(LATE)
            if c < CHUNKS - 2:
                n = CHUNK_BANKS[c] * BANK_TILES
                add_and_store(c, 0, n, q_rows, nc.gpsimd)
                add_and_store(c, 0, n, k_rows, nc.gpsimd)
        for c, units in ((CHUNKS - 2, PENULTIMATE_UNITS), (CHUNKS - 1, LAST_UNITS)):
            first = 0
            for n in units:
                add_and_store(c, first, n, q_rows, nc.vector)
                add_and_store(c, first, n, k_rows, nc.vector)
                first += n
